import numpy as np
import ml_dtypes


BF16 = ml_dtypes.bfloat16


def bf(x):
    return np.asarray(x, np.float32).astype(BF16)


def f64(x):
    return np.asarray(x).astype(np.float64)


E2M1 = np.array([0.0, 0.5, 1.0, 1.5, 2.0, 3.0, 4.0, 6.0, -0.0, -0.5, -1.0, -1.5, -2.0, -3.0, -4.0, -6.0])


def pack_weight(w, fmt):
    k, n = w.shape
    w = f64(bf(w)).reshape(k // 32, 32, n)
    amax = np.abs(w).max(1)
    if fmt == "e4m3":
        byte = np.frexp(amax)[1] - 1 + 127 - 7
    else:
        mant, ex = np.frexp(amax / 6.0)
        byte = np.where(mant > 0.5, ex, ex - 1) + 127
    byte = np.clip(np.where(amax > 0, byte, 1), 1, 254)
    scaled = (w * np.exp2(127.0 - byte)[:, None, :]).reshape(k, n).astype(np.float32)
    by_word = np.ascontiguousarray(scaled.reshape(k // 512, 128, 4, n).transpose(0, 1, 3, 2))
    if fmt == "e4m3":
        words = by_word.astype(ml_dtypes.float8_e4m3fn).view(np.uint8)
    else:
        c = by_word.astype(ml_dtypes.float4_e2m1fn).view(np.uint8) & 0xF
        words = c[..., 0::2] | (c[..., 1::2] << 4)
    return np.ascontiguousarray(words), np.ascontiguousarray(byte.astype(np.uint8).reshape(k // 512, 16, n))


def unpack_weight(words, scales, fmt):
    g, p, n, _ = words.shape
    if fmt == "e4m3":
        vals = np.ascontiguousarray(words).view(ml_dtypes.float8_e4m3fn).astype(np.float64)
    else:
        nib = np.empty((g, p, n, 4), np.uint8)
        nib[..., 0::2] = words & 0xF
        nib[..., 1::2] = words >> 4
        vals = E2M1[nib]
    vals = vals * np.repeat(np.exp2(scales.astype(np.float64) - 127.0), 8, axis=1)[..., None]
    return vals.transpose(0, 1, 3, 2).reshape(g * 512, n)

def pack4(w):
    words, scales = pack_weight(w, "e2m1")
    return words.reshape(words.shape[0], 128, -1), scales


def unpack4(words, scales):
    return unpack_weight(words.reshape(words.shape[0], 128, -1, 2), scales, "e2m1")


def kspread(k):
    return np.exp2(np.repeat(np.random.randint(-6, 7, k // 32), 32).astype(np.float64))


B, T, D, H, KV, DH = 2, 256, 1024, 16, 4, 128
THETA = 1000000.0
EPS = 1e-6
HALF = DH // 2


def rms_norm(u, w):
    return w * u / np.sqrt(np.mean(u * u, axis=-1, keepdims=True) + EPS)


def rope(u):
    timescale = THETA ** (2.0 * np.arange(HALF) / DH)
    ang = (np.arange(T)[:, None] / timescale[None, :])[None, :, None, :]
    sin, cos = np.sin(ang), np.cos(ang)
    a, b = u[..., :HALF], u[..., HALF:]
    return np.concatenate([a * cos - b * sin, b * cos + a * sin], axis=-1)


def setup_inputs():
    s = kspread(D)
    small = 3.0 * np.sqrt(EPS / D)
    x = np.random.standard_normal((B, T, D)) * s
    x_words, x_scales = pack4(x.reshape(B * T, D).T)
    wq_words, wq_scales = pack4(np.random.standard_normal((D, H * DH)) * small / s[:, None])
    wk_words, wk_scales = pack4(np.random.standard_normal((D, KV * DH)) * small / s[:, None])
    wv_words, wv_scales = pack4(np.random.standard_normal((D, KV * DH)) / np.sqrt(D) / s[:, None])
    q_norm_w = bf(1.0 + 0.1 * np.random.standard_normal(DH))
    k_norm_w = bf(1.0 + 0.1 * np.random.standard_normal(DH))
    return {"x_words": x_words, "x_scales": x_scales,
            "wq_words": wq_words, "wq_scales": wq_scales,
            "wk_words": wk_words, "wk_scales": wk_scales,
            "wv_words": wv_words, "wv_scales": wv_scales,
            "q_norm_w": q_norm_w,
            "k_norm_w": k_norm_w}


def reference(x_words, x_scales, wq_words, wq_scales, wk_words, wk_scales, wv_words, wv_scales, q_norm_w, k_norm_w):
    xq = unpack4(x_words, x_scales).T.reshape(B, T, D)
    q = (xq @ unpack4(wq_words, wq_scales)).reshape(B, T, H, DH)
    k = (xq @ unpack4(wk_words, wk_scales)).reshape(B, T, KV, DH)
    v = (xq @ unpack4(wv_words, wv_scales)).reshape(B, T, KV, DH)
    return rope(rms_norm(q, f64(q_norm_w))), rope(rms_norm(k, f64(k_norm_w))), v

@@ -1,0 +1,195 @@
+import math
+from contextlib import ExitStack
+
+import concourse.mybir as mybir
+
+F32 = mybir.dt.float32
+BF16 = mybir.dt.bfloat16
+I32 = mybir.dt.int32
+U8 = mybir.dt.uint8
+FP4X4 = mybir.dt.float4_e2m1fn_x4
+ACT = mybir.ActivationFunctionType
+ALU = mybir.AluOpType
+
+TOK, D, H, KV, DH = 512, 1024, 16, 4, 128
+NQ, NKV = H * DH, KV * DH
+HALF = DH // 2
+G = D // 512
+P = 128
+NB = 512
+HPB = NB // DH
+FLOPS = 2 * TOK * D * (NQ + 2 * NKV)
+
+
+def tile_qwen3attention_pa_kernel(tc, x_words, x_scales, wq_words, wq_scales, wk_words, wk_scales, wv_words, wv_scales, q_norm_w, k_norm_w, q_out, k_out, v_out):
+    nc = tc.nc
+    with ExitStack() as ctx:
+        keep = ctx.enter_context(tc.tile_pool(name="keep", bufs=1))
+        work = ctx.enter_context(tc.tile_pool(name="work", bufs=4))
+        psum = ctx.enter_context(tc.psum_pool(name="psum", bufs=8))
+
+        def codes_tile(cols, nm):
+            return keep.tile([P, G, 2 * cols], U8, name=nm, align_bytes=64)
+
+        def plane_tile(cols, nm):
+            return keep.tile([P, G, cols], U8, name=nm, align_bytes=64)
+
+        x_codes = codes_tile(TOK, "x_codes")
+        k_codes = codes_tile(NKV, "k_codes")
+        v_codes = codes_tile(NKV, "v_codes")
+        qa_codes = codes_tile(NQ // 2, "qa_codes")
+        qb_codes = codes_tile(NQ // 2, "qb_codes")
+        x_plane = plane_tile(TOK, "x_plane")
+        k_plane = plane_tile(NKV, "k_plane")
+        v_plane = plane_tile(NKV, "v_plane")
+        q_plane = plane_tile(NQ, "q_plane")
+
+        def load_codes(dst, src):
+            nc.sync.dma_start(out=dst[:], in_=src.rearrange("g p n -> p g n"))
+
+        def load_scales(plane, src):
+            for q in range(4):
+                nc.sync.dma_start(
+                    out=plane[32 * q : 32 * q + 4, :, :].bitcast(I32),
+                    in_=src[:, 4 * q : 4 * q + 4, :].rearrange("g r n -> r g n").bitcast(I32),
+                )
+
+        pos = keep.tile([P, 2], F32, name="pos")
+        freq = keep.tile([P, HALF], F32, name="freq")
+        zero = keep.tile([P, 1], F32, name="zero")
+        eps = keep.tile([P, 1], F32, name="eps")
+        wrow = keep.tile([P, 2 * DH], BF16, name="wrow")
+        ones = keep.tile([P, P], BF16, name="ones")
+
+        load_codes(x_codes, x_words)
+        load_codes(k_codes, wk_words)
+        nc.vector.memset(x_plane[:].bitcast(I32), 0)
+        nc.vector.memset(k_plane[:].bitcast(I32), 0)
+        load_scales(x_plane, x_scales)
+        load_scales(k_plane, wk_scales)
+
+        nc.vector.memset(zero[:], 0.0)
+        nc.gpsimd.iota(pos[:], pattern=[[P, 2]], base=0, channel_multiplier=1, allow_small_or_imprecise_dtypes=True)
+        ratio = 10.0 ** (-6.0 / HALF)
+        for j in range(4):
+            nc.vector.tensor_scalar(out=freq[:, j : j + 1], in0=zero[:], scalar1=1.0, scalar2=ratio**j / (2.0 * math.pi), op0=ALU.mult, op1=ALU.add)
+        n = 4
+        while n < HALF:
+            nc.vector.tensor_scalar(out=freq[:, n : 2 * n], in0=freq[:, 0:n], scalar1=ratio**n, scalar2=0.0, op0=ALU.mult, op1=ALU.add)
+            n *= 2
+        nc.gpsimd.memset(wrow[:], 0.0)
+        nc.gpsimd.memset(ones[:], 1.0)
+        nc.gpsimd.dma_start(out=wrow[0:1, 0:DH], in_=q_norm_w.rearrange("(o d) -> o d", o=1))
+        nc.gpsimd.dma_start(out=wrow[0:1, DH : 2 * DH], in_=k_norm_w.rearrange("(o d) -> o d", o=1))
+        nc.vector.memset(q_plane[:].bitcast(I32), 0)
+        nc.vector.memset(v_plane[:].bitcast(I32), 0)
+        nc.vector.tensor_scalar(out=eps[:], in0=zero[:], scalar1=1.0, scalar2=1e-6, op0=ALU.mult, op1=ALU.add)
+
+        load_codes(qa_codes, wq_words[:, :, 0:NQ])
+        load_scales(q_plane, wq_scales)
+        load_codes(qb_codes, wq_words[:, :, NQ : 2 * NQ])
+        load_codes(v_codes, wv_words)
+        load_scales(v_plane, wv_scales)
+
+        turns = keep.tile([P, 4, HALF], F32, name="turns")
+        whole = keep.tile([P, 4, HALF], I32, name="whole")
+        trig = keep.tile([P, 4, HALF], F32, name="trig")
+        for i in range(2):
+            nc.vector.tensor_scalar(out=turns[:, i, :], in0=freq[:], scalar1=pos[:, i : i + 1], scalar2=0.0, op0=ALU.mult, op1=ALU.add)
+        nc.vector.tensor_scalar(out=turns[:, 2:4, :], in0=turns[:, 0:2, :], scalar1=1.0, scalar2=0.25, op0=ALU.mult, op1=ALU.add)
+        nc.vector.tensor_copy(out=whole[:], in_=turns[:])
+        nc.vector.tensor_tensor(out=turns[:], in0=turns[:], in1=whole[:], op=ALU.subtract)
+        nc.scalar.activation(out=trig[:], in_=turns[:], func=ACT.Sin, scale=2.0 * math.pi)
+        warm = keep.tile([P, 1], F32, name="warm")
+        nc.scalar.activation(out=warm[:], in_=eps[:], func=ACT.Abs_reciprocal_sqrt, scale=1.0, bias=eps[:])
+
+        wb = psum.tile([P, NB], F32, tag="bank", name="wb")
+        nc.tensor.matmul(wb[:, 0 : 2 * DH], ones[:], wrow[:], start=True, stop=True)
+
+        def tables(lo, nm):
+            w = wb[:, lo : lo + DH]
+            c = keep.tile([P, 2, DH], F32, name="c_" + nm)
+            s = keep.tile([P, 2, DH], F32, name="s_" + nm)
+            nc.vector.tensor_tensor(
+                out=c[:].rearrange("p t (h j) -> p t h j", h=2),
+                in0=trig[:, 2:4, :].unsqueeze(2).to_broadcast([P, 2, 2, HALF]),
+                in1=w.rearrange("p (h j) -> p h j", h=2).unsqueeze(1).to_broadcast([P, 2, 2, HALF]),
+                op=ALU.mult,
+            )
+            nc.vector.scalar_tensor_tensor(
+                out=s[:, :, 0:HALF], in0=trig[:, 0:2, :], scalar=-1.0,
+                in1=w[:, HALF:DH].unsqueeze(1).to_broadcast([P, 2, HALF]), op0=ALU.mult, op1=ALU.mult,
+            )
+            nc.vector.tensor_tensor(
+                out=s[:, :, HALF:DH], in0=trig[:, 0:2, :],
+                in1=w[:, 0:HALF].unsqueeze(1).to_broadcast([P, 2, HALF]), op=ALU.mult,
+            )
+            return c, s
+
+        k_tab = tables(DH, "k")
+        q_tab = tables(0, "q")
+
+        def project(t, codes, code_lo, plane, plane_lo):
+            ps = psum.tile([P, NB], F32, tag="bank", name="bank")
+            for g in range(G):
+                nc.tensor.matmul_mx(
+                    out=ps[:],
+                    lhsT=x_codes[:, g, 2 * P * t : 2 * P * (t + 1)].bitcast(FP4X4),
+                    lhsT_scale=x_plane[:, g, P * t : P * (t + 1)],
+                    rhs=codes[:, g, 2 * code_lo : 2 * (code_lo + NB)].bitcast(FP4X4),
+                    rhs_scale=plane[:, g, plane_lo : plane_lo + NB],
+                    start=(g == 0),
+                    stop=(g == G - 1),
+                )
+            return ps
+
+        def rotate_store(t, ps, tab, dst):
+            c, s = tab
+            i = t % 2
+            junk = work.tile([P, NB], BF16, name="junk")
+            ss = work.tile([P, HPB], F32, name="ss")
+            r = work.tile([P, HPB], F32, name="r")
+            t1 = work.tile([P, NB], F32, name="t1")
+            t2 = work.tile([P, NB], F32, name="t2")
+            o = work.tile([P, NB], F32, name="o")
+            for h in range(HPB):
+                hc = slice(h * DH, (h + 1) * DH)
+                nc.scalar.activation(out=junk[:, hc], in_=ps[:, hc], func=ACT.Square, accum_out=ss[:, h : h + 1])
+            nc.scalar.activation(out=r[:], in_=ss[:], func=ACT.Abs_reciprocal_sqrt, scale=1.0 / DH, bias=eps[:])
+            for h in range(HPB):
+                hc = slice(h * DH, (h + 1) * DH)
+                nc.vector.scalar_tensor_tensor(out=t1[:, hc], in0=ps[:, hc], scalar=r[:, h : h + 1], in1=c[:, i, :], op0=ALU.mult, op1=ALU.mult)
+            for h in range(HPB):
+                hc = slice(h * DH, (h + 1) * DH)
+                nc.vector.scalar_tensor_tensor(
+                    out=t2[:, hc].rearrange("p (a j) -> p a j", a=2),
+                    in0=ps[:, hc].rearrange("p (a j) -> p a j", a=2)[:, ::-1, :],
+                    scalar=r[:, h : h + 1],
+                    in1=s[:, i, :].rearrange("p (a j) -> p a j", a=2),
+                    op0=ALU.mult, op1=ALU.mult,
+                )
+            nc.gpsimd.tensor_tensor(out=o[:], in0=t1[:], in1=t2[:], op=ALU.add)
+            nc.sync.dma_start(out=dst, in_=o[:])
+
+        def copy_store(ps, dst):
+            o = work.tile([P, NB], F32, name="ov")
+            nc.scalar.copy(out=o[:], in_=ps[:])
+            nc.sync.dma_start(out=dst, in_=o[:])
+
+        qf = q_out.rearrange("b t h d -> (b t) (h d)")
+        kf = k_out.rearrange("b t h d -> (b t) (h d)")
+        vf = v_out.rearrange("b t h d -> (b t) (h d)")
+        units = [("k", 0, t) for t in range(4)]
+        for b in range(4):
+            units += [("q", b, t) for t in range(4)]
+            units.append(("v", 0, b))
+        for kind, b, t in units:
+            rows = slice(P * t, P * (t + 1))
+            cols = slice(NB * b, NB * (b + 1))
+            if kind == "k":
+                rotate_store(t, project(t, k_codes, 0, k_plane, 0), k_tab, kf[rows, :])
+            elif kind == "v":
+                copy_store(project(t, v_codes, 0, v_plane, 0), vf[rows, :])
+            else:
+                codes = qa_codes if b < 2 else qb_codes
+                rotate_store(t, project(t, codes, NB * (b % 2), q_plane, NB * b), q_tab, qf[rows, cols])

@@ -2,6 +2,7 @@ import math
 from contextlib import ExitStack
 
 import concourse.mybir as mybir
+from concourse.masks import make_identity
 
 F32 = mybir.dt.float32
 BF16 = mybir.dt.bfloat16
@@ -25,7 +26,7 @@ def tile_qwen3attention_pa_kernel(tc, x_words, x_scales, wq_words, wq_scales, wk
     nc = tc.nc
     with ExitStack() as ctx:
         keep = ctx.enter_context(tc.tile_pool(name="keep", bufs=1))
-        work = ctx.enter_context(tc.tile_pool(name="work", bufs=4))
+        work = ctx.enter_context(tc.tile_pool(name="work", bufs=5))
         psum = ctx.enter_context(tc.psum_pool(name="psum", bufs=8))
 
         def codes_tile(cols, nm):
@@ -129,6 +130,9 @@ def tile_qwen3attention_pa_kernel(tc, x_words, x_scales, wq_words, wq_scales, wk
         k_tab = tables(DH, "k")
         q_tab = tables(0, "q")
 
+        ident = keep.tile([P, P], F32, name="ident")
+        make_identity(nc, ident[:])
+
         def project(t, codes, code_lo, plane, plane_lo):
             ps = psum.tile([P, NB], F32, tag="bank", name="bank")
             for g in range(G):
@@ -143,53 +147,113 @@ def tile_qwen3attention_pa_kernel(tc, x_words, x_scales, wq_words, wq_scales, wk
                 )
             return ps
 
-        def rotate_store(t, ps, tab, dst):
-            c, s = tab
-            i = t % 2
-            junk = work.tile([P, NB], BF16, name="junk")
-            ss = work.tile([P, HPB], F32, name="ss")
-            r = work.tile([P, HPB], F32, name="r")
-            t1 = work.tile([P, NB], F32, name="t1")
-            t2 = work.tile([P, NB], F32, name="t2")
-            o = work.tile([P, NB], F32, name="o")
-            for h in range(HPB):
-                hc = slice(h * DH, (h + 1) * DH)
-                nc.scalar.activation(out=junk[:, hc], in_=ps[:, hc], func=ACT.Square, accum_out=ss[:, h : h + 1])
-            nc.scalar.activation(out=r[:], in_=ss[:], func=ACT.Abs_reciprocal_sqrt, scale=1.0 / DH, bias=eps[:])
-            for h in range(HPB):
-                hc = slice(h * DH, (h + 1) * DH)
-                nc.vector.scalar_tensor_tensor(out=t1[:, hc], in0=ps[:, hc], scalar=r[:, h : h + 1], in1=c[:, i, :], op0=ALU.mult, op1=ALU.mult)
-            for h in range(HPB):
-                hc = slice(h * DH, (h + 1) * DH)
-                nc.vector.scalar_tensor_tensor(
-                    out=t2[:, hc].rearrange("p (a j) -> p a j", a=2),
-                    in0=ps[:, hc].rearrange("p (a j) -> p a j", a=2)[:, ::-1, :],
-                    scalar=r[:, h : h + 1],
-                    in1=s[:, i, :].rearrange("p (a j) -> p a j", a=2),
-                    op0=ALU.mult, op1=ALU.mult,
-                )
-            nc.gpsimd.tensor_tensor(out=o[:], in0=t1[:], in1=t2[:], op=ALU.add)
-            nc.sync.dma_start(out=dst, in_=o[:])
-
-        def copy_store(ps, dst):
-            o = work.tile([P, NB], F32, name="ov")
-            nc.scalar.copy(out=o[:], in_=ps[:])
-            nc.sync.dma_start(out=dst, in_=o[:])
-
         qf = q_out.rearrange("b t h d -> (b t) (h d)")
         kf = k_out.rearrange("b t h d -> (b t) (h d)")
         vf = v_out.rearrange("b t h d -> (b t) (h d)")
-        units = [("k", 0, t) for t in range(4)]
+        units = [("k", 0, t, "Bg1" if t < 3 else "Pp") for t in range(4)]
         for b in range(4):
-            units += [("q", b, t) for t in range(4)]
-            units.append(("v", 0, b))
-        for kind, b, t in units:
-            rows = slice(P * t, P * (t + 1))
-            cols = slice(NB * b, NB * (b + 1))
-            if kind == "k":
-                rotate_store(t, project(t, k_codes, 0, k_plane, 0), k_tab, kf[rows, :])
-            elif kind == "v":
-                copy_store(project(t, v_codes, 0, v_plane, 0), vf[rows, :])
+            units.append(("v", 0, b, ""))
+            units += [("q", b, t, "Bv2" if (b, t) == (3, 3) else "Pp" if (t == 3) else "Bg1") for t in range(4)]
+        heads = [slice(h * DH, (h + 1) * DH) for h in range(HPB)]
+
+        def halves(ap):
+            return ap.rearrange("p (a j) -> p a j", a=2)
+
+        def dest(u):
+            kind, b, t, form = u
+            flat = {"k": kf, "q": qf, "v": vf}[kind]
+            return flat[P * t : P * (t + 1), NB * b : NB * (b + 1)]
+
+        def do_project(n):
+            kind, b, t, form = units[n]
+            if kind == "v":
+                st[n]["ps"] = project(t, v_codes, 0, v_plane, 0)
+            elif kind == "k":
+                st[n]["ps"] = project(t, k_codes, 0, k_plane, 0)
             else:
-                codes = qa_codes if b < 2 else qb_codes
-                rotate_store(t, project(t, codes, NB * (b % 2), q_plane, NB * b), q_tab, qf[rows, cols])
+                st[n]["ps"] = project(t, qa_codes if b < 2 else qb_codes, NB * (b % 2), q_plane, NB * b)
+
+        def do_norms(n):
+            ps = st[n]["ps"]
+            if units[n][0] == "v":
+                ov = work.tile([P, NB], F32, name="ov")
+                nc.scalar.copy(out=ov[:], in_=ps[:])
+                nc.sync.dma_start(out=dest(units[n]), in_=ov[:])
+                return
+            junk = work.tile([P, NB], BF16, name="junk")
+            ss = work.tile([P, HPB], F32, name="ss")
+            r = work.tile([P, HPB], F32, name="r", bufs=12)
+            for h in range(HPB):
+                nc.scalar.activation(out=junk[:, heads[h]], in_=ps[:, heads[h]], func=ACT.Square, accum_out=ss[:, h : h + 1])
+            nc.scalar.activation(out=r[:], in_=ss[:], func=ACT.Abs_reciprocal_sqrt, scale=1.0 / DH, bias=eps[:])
+            st[n]["r"] = r
+
+        def do_rotate(n):
+            kind, b, t, form = units[n]
+            if kind == "v":
+                return
+            ps, r, i = st[n]["ps"], st[n]["r"], t % 2
+            c, s = k_tab if kind == "k" else q_tab
+            t1 = work.tile([P, NB], F32, name="t1")
+            t2 = work.tile([P, NB], F32, name="t2")
+            st[n]["t"] = (t1, t2)
+            if form[0] in "PW":
+                nc.vector.tensor_tensor(
+                    out=t1[:].rearrange("p (h d) -> p h d", h=HPB), in0=ps[:].rearrange("p (h d) -> p h d", h=HPB),
+                    in1=c[:, i, :].unsqueeze(1).to_broadcast([P, HPB, DH]), op=ALU.mult,
+                )
+                nc.vector.tensor_tensor(
+                    out=t2[:].rearrange("p (h a j) -> p h a j", h=HPB, a=2),
+                    in0=ps[:].rearrange("p (h a j) -> p h a j", h=HPB, a=2)[:, :, ::-1, :],
+                    in1=halves(s[:, i, :]).unsqueeze(1).to_broadcast([P, HPB, 2, HALF]), op=ALU.mult,
+                )
+            else:
+                for h in range(HPB):
+                    nc.vector.scalar_tensor_tensor(out=t1[:, heads[h]], in0=ps[:, heads[h]], scalar=r[:, h : h + 1], in1=c[:, i, :], op0=ALU.mult, op1=ALU.mult)
+                for h in range(HPB):
+                    nc.vector.scalar_tensor_tensor(
+                        out=halves(t2[:, heads[h]]), in0=halves(ps[:, heads[h]])[:, ::-1, :],
+                        scalar=r[:, h : h + 1], in1=halves(s[:, i, :]), op0=ALU.mult, op1=ALU.mult,
+                    )
+
+        def do_add(n):
+            kind, b, t, form = units[n]
+            if kind == "v" or form[0] == "P":
+                return
+            t1, t2 = st[n]["t"]
+            o = work.tile([P, NB], F32, name="o")
+            st[n]["o"] = o
+            adder = nc.vector if form[1] == "v" else nc.gpsimd
+            parts = int(form[2:])
+            w = NB // parts
+            for k in range(parts):
+                kc = slice(k * w, (k + 1) * w)
+                adder.tensor_tensor(out=o[:, kc], in0=t1[:, kc], in1=t2[:, kc], op=ALU.add)
+                if form[0] == "B":
+                    nc.sync.dma_start(out=dest(units[n])[:, kc], in_=o[:, kc])
+
+        def do_padd(n):
+            if units[n][3][:1] != "P":
+                return
+            t1, t2 = st[n]["t"]
+            acc = psum.tile([P, NB], F32, tag="bank", name="acc")
+            nc.tensor.matmul(acc[:], ident[:], t1[:], start=True, stop=False)
+            nc.tensor.matmul(acc[:], ident[:], t2[:], start=False, stop=True)
+            st[n]["o"] = acc
+
+        def do_finish(n):
+            if units[n][3][:1] not in ("P", "W"):
+                return
+            src, r = st[n]["o"], st[n]["r"]
+            o2 = work.tile([P, NB], F32, name="o2")
+            for h in range(HPB):
+                nc.scalar.activation(out=o2[:, heads[h]], in_=src[:, heads[h]], func=ACT.Copy, scale=r[:, h : h + 1])
+            nc.sync.dma_start(out=dest(units[n]), in_=o2[:])
+
+        N = len(units)
+        st = [{} for u in units]
+        stages = ((do_project, 4), (do_norms, 1), (do_rotate, 0), (do_add, 0), (do_padd, -1), (do_finish, -3))
+        for step in range(-4, N + 3):
+            for fn, shift in stages:
+                if 0 <= step + shift < N:
+                    fn(step + shift)

@@ -80,8 +80,8 @@ def tile_qwen3attention_pa_kernel(tc, x_words, x_scales, wq_words, wq_scales, wk
             n *= 2
         nc.gpsimd.memset(wrow[:], 0.0)
         nc.gpsimd.memset(ones[:], 1.0)
-        nc.gpsimd.dma_start(out=wrow[0:1, 0:DH], in_=q_norm_w.rearrange("(o d) -> o d", o=1))
         nc.gpsimd.dma_start(out=wrow[0:1, DH : 2 * DH], in_=k_norm_w.rearrange("(o d) -> o d", o=1))
+        nc.gpsimd.dma_start(out=wrow[0:1, 0:DH], in_=q_norm_w.rearrange("(o d) -> o d", o=1))
         nc.vector.memset(q_plane[:].bitcast(I32), 0)
         nc.vector.memset(v_plane[:].bitcast(I32), 0)
         nc.vector.tensor_scalar(out=eps[:], in0=zero[:], scalar1=1.0, scalar2=1e-6, op0=ALU.mult, op1=ALU.add)
@@ -105,7 +105,7 @@ def tile_qwen3attention_pa_kernel(tc, x_words, x_scales, wq_words, wq_scales, wk
         nc.scalar.activation(out=warm[:], in_=eps[:], func=ACT.Abs_reciprocal_sqrt, scale=1.0, bias=eps[:])
 
         wb = psum.tile([P, NB], F32, tag="bank", name="wb")
-        nc.tensor.matmul(wb[:, 0 : 2 * DH], ones[:], wrow[:], start=True, stop=True)
+        nc.tensor.matmul(wb[:, DH : 2 * DH], ones[:], wrow[:, DH : 2 * DH], start=True, stop=True)
 
         def tables(lo, nm):
             w = wb[:, lo : lo + DH]
@@ -128,7 +128,6 @@ def tile_qwen3attention_pa_kernel(tc, x_words, x_scales, wq_words, wq_scales, wk
             return c, s
 
         k_tab = tables(DH, "k")
-        q_tab = tables(0, "q")
 
         ident = keep.tile([P, P], F32, name="ident")
         make_identity(nc, ident[:])
@@ -150,10 +149,13 @@ def tile_qwen3attention_pa_kernel(tc, x_words, x_scales, wq_words, wq_scales, wk
         qf = q_out.rearrange("b t h d -> (b t) (h d)")
         kf = k_out.rearrange("b t h d -> (b t) (h d)")
         vf = v_out.rearrange("b t h d -> (b t) (h d)")
-        units = [("k", 0, t, "Bg1" if t < 3 else "Pp") for t in range(4)]
-        for b in range(4):
-            units.append(("v", 0, b, ""))
-            units += [("q", b, t, "Bv2" if (b, t) == (3, 3) else "Pp" if (t == 3) else "Bg1") for t in range(4)]
+        units = [("k", 0, t, "Pp" if t == 0 else "Bg1") for t in range(4)]
+        units += [("q", 0, t, "Pp" if t == 2 else "Bg1") for t in range(4)]
+        units += [("q", 1, t, "Pp" if t == 2 else "Bg1") for t in range(4)]
+        units += [("v", 0, 0, ""), ("v", 0, 1, "")]
+        units += [("q", 2, t, "Pp" if t == 2 else "Bg1") for t in range(4)]
+        units += [("v", 0, 2, ""), ("v", 0, 3, "")]
+        units += [("q", 3, t, "Bv2" if t == 3 else "Bg1") for t in range(4)]
         heads = [slice(h * DH, (h + 1) * DH) for h in range(HPB)]
 
         def halves(ap):
@@ -192,7 +194,7 @@ def tile_qwen3attention_pa_kernel(tc, x_words, x_scales, wq_words, wq_scales, wk
             kind, b, t, form = units[n]
             if kind == "v":
                 return
-            ps, r, i = st[n]["ps"], st[n]["r"], t % 2
+            ps, i = st[n]["ps"], t % 2
             c, s = k_tab if kind == "k" else q_tab
             t1 = work.tile([P, NB], F32, name="t1")
             t2 = work.tile([P, NB], F32, name="t2")
@@ -208,6 +210,7 @@ def tile_qwen3attention_pa_kernel(tc, x_words, x_scales, wq_words, wq_scales, wk
                     in1=halves(s[:, i, :]).unsqueeze(1).to_broadcast([P, HPB, 2, HALF]), op=ALU.mult,
                 )
             else:
+                r = st[n]["r"]
                 for h in range(HPB):
                     nc.vector.scalar_tensor_tensor(out=t1[:, heads[h]], in0=ps[:, heads[h]], scalar=r[:, h : h + 1], in1=c[:, i, :], op0=ALU.mult, op1=ALU.mult)
                 for h in range(HPB):
@@ -252,8 +255,27 @@ def tile_qwen3attention_pa_kernel(tc, x_words, x_scales, wq_words, wq_scales, wk
 
         N = len(units)
         st = [{} for u in units]
-        stages = ((do_project, 4), (do_norms, 1), (do_rotate, 0), (do_add, 0), (do_padd, -1), (do_finish, -3))
-        for step in range(-4, N + 3):
-            for fn, shift in stages:
-                if 0 <= step + shift < N:
-                    fn(step + shift)
+        LEAD, AHEAD, FIN = 5, 2, 3
+        for n in range(3):
+            do_project(n)
+        nc.tensor.matmul(wb[:, 0:DH], ones[:], wrow[:, 0:DH], start=True, stop=True)
+        q_tab = tables(0, "q")
+        for n in range(3, LEAD):
+            do_project(n)
+        for n in range(1, AHEAD):
+            do_norms(n)
+        for n in range(N + FIN):
+            if n + LEAD < N:
+                do_project(n + LEAD)
+            if n == 0:
+                do_rotate(n)
+                do_norms(n)
+            if n + AHEAD < N:
+                do_norms(n + AHEAD)
+            if 0 < n < N:
+                do_rotate(n)
+                do_add(n)
+            if 0 <= n - 1 < N:
+                do_padd(n - 1)
+            if 0 <= n - FIN < N:
+                do_finish(n - FIN)

import math
from contextlib import ExitStack

import concourse.mybir as mybir
from concourse.masks import make_identity

F32 = mybir.dt.float32
BF16 = mybir.dt.bfloat16
I32 = mybir.dt.int32
U8 = mybir.dt.uint8
FP4X4 = mybir.dt.float4_e2m1fn_x4
ACT = mybir.ActivationFunctionType
ALU = mybir.AluOpType

TOK, D, H, KV, DH = 512, 1024, 16, 4, 128
NQ, NKV = H * DH, KV * DH
HALF = DH // 2
G = D // 512
P = 128
NB = 512
HPB = NB // DH
FLOPS = 2 * TOK * D * (NQ + 2 * NKV)


def tile_qwen3attention_pa_kernel(tc, x_words, x_scales, wq_words, wq_scales, wk_words, wk_scales, wv_words, wv_scales, q_norm_w, k_norm_w, q_out, k_out, v_out):
    nc = tc.nc
    with ExitStack() as ctx:
        keep = ctx.enter_context(tc.tile_pool(name="keep", bufs=1))
        work = ctx.enter_context(tc.tile_pool(name="work", bufs=5))
        psum = ctx.enter_context(tc.psum_pool(name="psum", bufs=8))

        def codes_tile(cols, nm):
            return keep.tile([P, G, 2 * cols], U8, name=nm, align_bytes=64)

        def plane_tile(cols, nm):
            return keep.tile([P, G, cols], U8, name=nm, align_bytes=64)

        x_codes = codes_tile(TOK, "x_codes")
        k_codes = codes_tile(NKV, "k_codes")
        v_codes = codes_tile(NKV, "v_codes")
        qa_codes = codes_tile(NQ // 2, "qa_codes")
        qb_codes = codes_tile(NQ // 2, "qb_codes")
        x_plane = plane_tile(TOK, "x_plane")
        k_plane = plane_tile(NKV, "k_plane")
        v_plane = plane_tile(NKV, "v_plane")
        q_plane = plane_tile(NQ, "q_plane")

        def load_codes(dst, src):
            nc.sync.dma_start(out=dst[:], in_=src.rearrange("g p n -> p g n"))

        def load_scales(plane, src):
            for q in range(4):
                nc.sync.dma_start(
                    out=plane[32 * q : 32 * q + 4, :, :].bitcast(I32),
                    in_=src[:, 4 * q : 4 * q + 4, :].rearrange("g r n -> r g n").bitcast(I32),
                )

        pos = keep.tile([P, 2], F32, name="pos")
        freq = keep.tile([P, HALF], F32, name="freq")
        zero = keep.tile([P, 1], F32, name="zero")
        eps = keep.tile([P, 1], F32, name="eps")
        wrow = keep.tile([P, 2 * DH], BF16, name="wrow")
        ones = keep.tile([P, P], BF16, name="ones")

        load_codes(x_codes, x_words)
        load_codes(k_codes, wk_words)
        nc.vector.memset(x_plane[:].bitcast(I32), 0)
        nc.vector.memset(k_plane[:].bitcast(I32), 0)
        load_scales(x_plane, x_scales)
        load_scales(k_plane, wk_scales)

        nc.vector.memset(zero[:], 0.0)
        nc.gpsimd.iota(pos[:], pattern=[[P, 2]], base=0, channel_multiplier=1, allow_small_or_imprecise_dtypes=True)
        ratio = 10.0 ** (-6.0 / HALF)
        for j in range(4):
            nc.vector.tensor_scalar(out=freq[:, j : j + 1], in0=zero[:], scalar1=1.0, scalar2=ratio**j / (2.0 * math.pi), op0=ALU.mult, op1=ALU.add)
        n = 4
        while n < HALF:
            nc.vector.tensor_scalar(out=freq[:, n : 2 * n], in0=freq[:, 0:n], scalar1=ratio**n, scalar2=0.0, op0=ALU.mult, op1=ALU.add)
            n *= 2
        nc.gpsimd.memset(wrow[:], 0.0)
        nc.gpsimd.memset(ones[:], 1.0)
        nc.gpsimd.dma_start(out=wrow[0:1, DH : 2 * DH], in_=k_norm_w.rearrange("(o d) -> o d", o=1))
        nc.gpsimd.dma_start(out=wrow[0:1, 0:DH], in_=q_norm_w.rearrange("(o d) -> o d", o=1))
        nc.vector.memset(q_plane[:].bitcast(I32), 0)
        nc.vector.memset(v_plane[:].bitcast(I32), 0)
        nc.vector.tensor_scalar(out=eps[:], in0=zero[:], scalar1=1.0, scalar2=1e-6, op0=ALU.mult, op1=ALU.add)

        load_codes(qa_codes, wq_words[:, :, 0:NQ])
        load_scales(q_plane, wq_scales)
        load_codes(qb_codes, wq_words[:, :, NQ : 2 * NQ])
        load_codes(v_codes, wv_words)
        load_scales(v_plane, wv_scales)

        turns = keep.tile([P, 4, HALF], F32, name="turns")
        whole = keep.tile([P, 4, HALF], I32, name="whole")
        trig = keep.tile([P, 4, HALF], F32, name="trig")
        for i in range(2):
            nc.vector.tensor_scalar(out=turns[:, i, :], in0=freq[:], scalar1=pos[:, i : i + 1], scalar2=0.0, op0=ALU.mult, op1=ALU.add)
        nc.vector.tensor_scalar(out=turns[:, 2:4, :], in0=turns[:, 0:2, :], scalar1=1.0, scalar2=0.25, op0=ALU.mult, op1=ALU.add)
        nc.vector.tensor_copy(out=whole[:], in_=turns[:])
        nc.vector.tensor_tensor(out=turns[:], in0=turns[:], in1=whole[:], op=ALU.subtract)
        nc.scalar.activation(out=trig[:], in_=turns[:], func=ACT.Sin, scale=2.0 * math.pi)
        warm = keep.tile([P, 1], F32, name="warm")
        nc.scalar.activation(out=warm[:], in_=eps[:], func=ACT.Abs_reciprocal_sqrt, scale=1.0, bias=eps[:])

        wb = psum.tile([P, NB], F32, tag="bank", name="wb")
        nc.tensor.matmul(wb[:, DH : 2 * DH], ones[:], wrow[:, DH : 2 * DH], start=True, stop=True)

        def tables(lo, nm):
            w = wb[:, lo : lo + DH]
            c = keep.tile([P, 2, DH], F32, name="c_" + nm)
            s = keep.tile([P, 2, DH], F32, name="s_" + nm)
            nc.vector.tensor_tensor(
                out=c[:].rearrange("p t (h j) -> p t h j", h=2),
                in0=trig[:, 2:4, :].unsqueeze(2).to_broadcast([P, 2, 2, HALF]),
                in1=w.rearrange("p (h j) -> p h j", h=2).unsqueeze(1).to_broadcast([P, 2, 2, HALF]),
                op=ALU.mult,
            )
            nc.vector.scalar_tensor_tensor(
                out=s[:, :, 0:HALF], in0=trig[:, 0:2, :], scalar=-1.0,
                in1=w[:, HALF:DH].unsqueeze(1).to_broadcast([P, 2, HALF]), op0=ALU.mult, op1=ALU.mult,
            )
            nc.vector.tensor_tensor(
                out=s[:, :, HALF:DH], in0=trig[:, 0:2, :],
                in1=w[:, 0:HALF].unsqueeze(1).to_broadcast([P, 2, HALF]), op=ALU.mult,
            )
            return c, s

        k_tab = tables(DH, "k")

        ident = keep.tile([P, P], F32, name="ident")
        make_identity(nc, ident[:])

        def project(t, codes, code_lo, plane, plane_lo):
            ps = psum.tile([P, NB], F32, tag="bank", name="bank")
            for g in range(G):
                nc.tensor.matmul_mx(
                    out=ps[:],
                    lhsT=x_codes[:, g, 2 * P * t : 2 * P * (t + 1)].bitcast(FP4X4),
                    lhsT_scale=x_plane[:, g, P * t : P * (t + 1)],
                    rhs=codes[:, g, 2 * code_lo : 2 * (code_lo + NB)].bitcast(FP4X4),
                    rhs_scale=plane[:, g, plane_lo : plane_lo + NB],
                    start=(g == 0),
                    stop=(g == G - 1),
                )
            return ps

        qf = q_out.rearrange("b t h d -> (b t) (h d)")
        kf = k_out.rearrange("b t h d -> (b t) (h d)")
        vf = v_out.rearrange("b t h d -> (b t) (h d)")
        units = [("k", 0, t, "Pp" if t == 0 else "Bg1") for t in range(4)]
        units += [("q", 0, t, "Pp" if t == 2 else "Bg1") for t in range(4)]
        units += [("q", 1, t, "Pp" if t == 2 else "Bg1") for t in range(4)]
        units += [("v", 0, 0, ""), ("v", 0, 1, "")]
        units += [("q", 2, t, "Pp" if t == 2 else "Bg1") for t in range(4)]
        units += [("v", 0, 2, ""), ("v", 0, 3, "")]
        units += [("q", 3, t, "Bv2" if t == 3 else "Bg1") for t in range(4)]
        heads = [slice(h * DH, (h + 1) * DH) for h in range(HPB)]

        def halves(ap):
            return ap.rearrange("p (a j) -> p a j", a=2)

        def dest(u):
            kind, b, t, form = u
            flat = {"k": kf, "q": qf, "v": vf}[kind]
            return flat[P * t : P * (t + 1), NB * b : NB * (b + 1)]

        def do_project(n):
            kind, b, t, form = units[n]
            if kind == "v":
                st[n]["ps"] = project(t, v_codes, 0, v_plane, 0)
            elif kind == "k":
                st[n]["ps"] = project(t, k_codes, 0, k_plane, 0)
            else:
                st[n]["ps"] = project(t, qa_codes if b < 2 else qb_codes, NB * (b % 2), q_plane, NB * b)

        def do_norms(n):
            ps = st[n]["ps"]
            if units[n][0] == "v":
                ov = work.tile([P, NB], F32, name="ov")
                nc.scalar.copy(out=ov[:], in_=ps[:])
                nc.sync.dma_start(out=dest(units[n]), in_=ov[:])
                return
            junk = work.tile([P, NB], BF16, name="junk")
            ss = work.tile([P, HPB], F32, name="ss")
            r = work.tile([P, HPB], F32, name="r", bufs=12)
            for h in range(HPB):
                nc.scalar.activation(out=junk[:, heads[h]], in_=ps[:, heads[h]], func=ACT.Square, accum_out=ss[:, h : h + 1])
            nc.scalar.activation(out=r[:], in_=ss[:], func=ACT.Abs_reciprocal_sqrt, scale=1.0 / DH, bias=eps[:])
            st[n]["r"] = r

        def do_rotate(n):
            kind, b, t, form = units[n]
            if kind == "v":
                return
            ps, i = st[n]["ps"], t % 2
            c, s = k_tab if kind == "k" else q_tab
            t1 = work.tile([P, NB], F32, name="t1")
            t2 = work.tile([P, NB], F32, name="t2")
            st[n]["t"] = (t1, t2)
            if form[0] in "PW":
                nc.vector.tensor_tensor(
                    out=t1[:].rearrange("p (h d) -> p h d", h=HPB), in0=ps[:].rearrange("p (h d) -> p h d", h=HPB),
                    in1=c[:, i, :].unsqueeze(1).to_broadcast([P, HPB, DH]), op=ALU.mult,
                )
                nc.vector.tensor_tensor(
                    out=t2[:].rearrange("p (h a j) -> p h a j", h=HPB, a=2),
                    in0=ps[:].rearrange("p (h a j) -> p h a j", h=HPB, a=2)[:, :, ::-1, :],
                    in1=halves(s[:, i, :]).unsqueeze(1).to_broadcast([P, HPB, 2, HALF]), op=ALU.mult,
                )
            else:
                r = st[n]["r"]
                for h in range(HPB):
                    nc.vector.scalar_tensor_tensor(out=t1[:, heads[h]], in0=ps[:, heads[h]], scalar=r[:, h : h + 1], in1=c[:, i, :], op0=ALU.mult, op1=ALU.mult)
                for h in range(HPB):
                    nc.vector.scalar_tensor_tensor(
                        out=halves(t2[:, heads[h]]), in0=halves(ps[:, heads[h]])[:, ::-1, :],
                        scalar=r[:, h : h + 1], in1=halves(s[:, i, :]), op0=ALU.mult, op1=ALU.mult,
                    )

        def do_add(n):
            kind, b, t, form = units[n]
            if kind == "v" or form[0] == "P":
                return
            t1, t2 = st[n]["t"]
            o = work.tile([P, NB], F32, name="o")
            st[n]["o"] = o
            adder = nc.vector if form[1] == "v" else nc.gpsimd
            parts = int(form[2:])
            w = NB // parts
            for k in range(parts):
                kc = slice(k * w, (k + 1) * w)
                adder.tensor_tensor(out=o[:, kc], in0=t1[:, kc], in1=t2[:, kc], op=ALU.add)
                if form[0] == "B":
                    nc.sync.dma_start(out=dest(units[n])[:, kc], in_=o[:, kc])

        def do_padd(n):
            if units[n][3][:1] != "P":
                return
            t1, t2 = st[n]["t"]
            acc = psum.tile([P, NB], F32, tag="bank", name="acc")
            nc.tensor.matmul(acc[:], ident[:], t1[:], start=True, stop=False)
            nc.tensor.matmul(acc[:], ident[:], t2[:], start=False, stop=True)
            st[n]["o"] = acc

        def do_finish(n):
            if units[n][3][:1] not in ("P", "W"):
                return
            src, r = st[n]["o"], st[n]["r"]
            o2 = work.tile([P, NB], F32, name="o2")
            for h in range(HPB):
                nc.scalar.activation(out=o2[:, heads[h]], in_=src[:, heads[h]], func=ACT.Copy, scale=r[:, h : h + 1])
            nc.sync.dma_start(out=dest(units[n]), in_=o2[:])

        N = len(units)
        st = [{} for u in units]
        LEAD, AHEAD, FIN = 5, 2, 3
        for n in range(3):
            do_project(n)
        nc.tensor.matmul(wb[:, 0:DH], ones[:], wrow[:, 0:DH], start=True, stop=True)
        q_tab = tables(0, "q")
        for n in range(3, LEAD):
            do_project(n)
        for n in range(1, AHEAD):
            do_norms(n)
        for n in range(N + FIN):
            if n + LEAD < N:
                do_project(n + LEAD)
            if n == 0:
                do_rotate(n)
                do_norms(n)
            if n + AHEAD < N:
                do_norms(n + AHEAD)
            if 0 < n < N:
                do_rotate(n)
                do_add(n)
            if 0 <= n - 1 < N:
                do_padd(n - 1)
            if 0 <= n - FIN < N:
                do_finish(n - FIN)
